import numpy as np
import ml_dtypes


def mxq(x, axis, fmt="e4m3"):
    dtype, down = {"e4m3": (ml_dtypes.float8_e4m3fn, 7), "e5m2": (ml_dtypes.float8_e5m2, 14)}[fmt]
    v = np.moveaxis(np.asarray(x, np.float32).astype(ml_dtypes.bfloat16).astype(np.float64), axis, -1)
    blocks = v.reshape(v.shape[:-1] + (-1, 32))
    amax = np.abs(blocks).max(-1, keepdims=True)
    byte = np.maximum(np.where(amax > 0, np.frexp(amax)[1] - 1 + 127, 0) - down, 1)
    scale = np.exp2(byte - 127.0)
    codes = (blocks / scale).astype(np.float32).astype(dtype).astype(np.float64)
    return np.moveaxis((codes * scale).reshape(v.shape), -1, axis)


WIDE = False


def mx_kscale(k):
    if not WIDE:
        return np.ones(k)
    levels = np.array([10, -10, 5, -5, 0])
    if k % 512:
        return np.exp2(np.random.permutation(np.resize(levels, k // 32))).repeat(32)
    a = np.empty((k // 512, 16))
    for p in range(k // 512):
        a[p, :8] = np.random.permutation(np.resize(levels, 8))
        for g in range(8):
            far = levels[np.abs(levels - a[p, g]) >= 10]
            a[p, g + 8] = far[np.random.randint(len(far))]
    return np.exp2(a.ravel()).repeat(32)


BF16 = ml_dtypes.bfloat16


def bf(x):
    return np.asarray(x, np.float32).astype(BF16)


def f64(x):
    return np.asarray(x).astype(np.float64)


B, D, F = 8192, 512, 2560
EPS = 1e-12


def l2_gain_norm(h, g):
    n = np.sqrt((h * h).sum(-1, keepdims=True))
    return h / np.maximum(n, EPS) * (D ** -0.5) * g


def setup_inputs():
    s = mx_kscale(D)
    r = np.random.standard_normal
    return {"x": bf(r((B, D))),
            "state": bf(r((B, D))),
            "g1": bf(D * (1.0 + 0.1 * r(D)) * s),
            "wv": bf(r((D, D)) / np.sqrt(D) / s[None, :]),
            "bv": bf(0.2 * r(D))}


def reference(x, state, g1, wv, bv):
    h = f64(x) + f64(state)
    hn = l2_gain_norm(h, f64(g1))
    return (mxq(hn, 1, "e4m3") @ mxq(f64(wv), 1, "e4m3").T) + f64(bv)

@@ -1,0 +1,219 @@
+from contextlib import ExitStack
+
+import concourse.mybir as mybir
+from concourse.masks import make_identity
+
+F32 = mybir.dt.float32
+BF16 = mybir.dt.bfloat16
+U32 = mybir.dt.uint32
+U8 = mybir.dt.uint8
+FP8X4 = mybir.dt.float8_e4m3fn_x4
+ACT = mybir.ActivationFunctionType
+ALU = mybir.AluOpType
+
+P = 128
+PACK = 4
+D = P * PACK
+B = 8192
+EPS = 1e-12
+TILES = 4
+GROUP_ROWS = P * TILES
+GROUPS = B // GROUP_ROWS
+LOADS_AHEAD = 4
+ADD_TILES = 2
+VECTOR_ADDS = 3
+STORE_TILES = 2
+
+NORMALISE_LAG = 1
+GAIN_LAG = 2
+PRODUCT_LAG = 3
+
+FLOPS = 2 * B * D * D
+
+
+def tile_recurrenttransformerblock_pa_t_kernel(tc, x, state, g1, wv, bv, out):
+    nc = tc.nc
+
+    def group_view(dram, g):
+        rows = dram[g * GROUP_ROWS : (g + 1) * GROUP_ROWS, :]
+        return rows.rearrange("(p t) k -> p t k", t=TILES)
+
+    with ExitStack() as ctx:
+        const = ctx.enter_context(tc.tile_pool(name="const", bufs=1))
+        inputs = ctx.enter_context(tc.tile_pool(name="inputs", bufs=LOADS_AHEAD + 1))
+        sums = ctx.enter_context(tc.tile_pool(name="sums", bufs=3))
+        stats = ctx.enter_context(tc.tile_pool(name="stats", bufs=3))
+        results = ctx.enter_context(tc.tile_pool(name="results", bufs=3))
+        scaled = ctx.enter_context(tc.tile_pool(name="scaled", bufs=2))
+        packed = ctx.enter_context(tc.tile_pool(name="packed", bufs=2))
+        turned = ctx.enter_context(tc.psum_pool(name="turned", bufs=TILES))
+        products = ctx.enter_context(tc.psum_pool(name="products", bufs=TILES))
+        ctx.enter_context(tc.manual_schedule())
+
+        x_rows, s_rows, h, sum_sq, excess, inv_norm, h_unit, h_turned = {}, {}, {}, {}, {}, {}, {}, {}
+        hn_words, hn_codes, hn_scales, v_sums = {}, {}, {}, {}
+
+        def load(g):
+            x_rows[g] = inputs.tile([P, TILES, D], BF16, name="x_rows")
+            s_rows[g] = inputs.tile([P, TILES, D], BF16, name="s_rows")
+            nc.sync.dma_start(out=x_rows[g][:], in_=group_view(x, g))
+            nc.sync.dma_start(out=s_rows[g][:], in_=group_view(state, g))
+
+        def add_inputs(g):
+            engine = nc.vector if g < VECTOR_ADDS else nc.gpsimd
+            h[g] = sums.tile([P, TILES, D], F32, name="h")
+            for t in range(0, TILES, ADD_TILES):
+                part = slice(t, t + ADD_TILES)
+                engine.tensor_tensor(
+                    out=h[g][:, part, :], in0=x_rows[g][:, part, :], in1=s_rows[g][:, part, :], op=ALU.add
+                )
+
+        for g in range(LOADS_AHEAD):
+            load(g)
+
+        ident_f32 = const.tile([P, P], F32)
+        make_identity(nc, ident_f32[:])
+        ident_bf16 = const.tile([P, P], BF16)
+        make_identity(nc, ident_bf16[:])
+
+        one = const.tile([P, 1], F32)
+        nc.vector.memset(one[:], 1.0)
+        warm = const.tile([P, 1], F32)
+        nc.scalar.activation(out=warm[:], in_=one[:], func=ACT.Abs_reciprocal_sqrt)
+
+        g_words = const.tile([P, PACK], BF16)
+        nc.sync.dma_start(out=g_words[:], in_=g1.rearrange("(p c) -> p c", c=PACK))
+        w_rows = const.tile([P, PACK, D], BF16)
+        nc.sync.dma_start(out=w_rows[:], in_=wv.rearrange("(b p) k -> p b k", p=P))
+        bias_rows = const.tile([P, D], BF16)
+        nc.sync.dma_start(out=bias_rows[:], in_=bv.partition_broadcast(P))
+
+        for g in range(VECTOR_ADDS):
+            add_inputs(g)
+
+        gain_by_k = const.tile([P, PACK], F32)
+        nc.vector.tensor_copy(out=gain_by_k[:], in_=g_words[:])
+
+        w_words = const.tile([P, D, PACK], BF16, align_bytes=64)
+        for b in range(PACK):
+            w_turned = turned.tile([P, PACK, P], BF16, tag="turned")
+            for c in range(PACK):
+                nc.tensor.transpose(w_turned[:, c, :], w_rows[:, b, c:D:PACK], ident_bf16[:])
+            nc.vector.tensor_copy(
+                out=w_words[:, b * P : (b + 1) * P, :], in_=w_turned[:].rearrange("p c n -> p n c")
+            )
+        w_codes = const.tile([P, D], U32, align_bytes=64)
+        w_scales = const.tile([P, D], U8, align_bytes=64)
+        nc.vector.quantize_mx(
+            out=w_codes[:].bitcast(FP8X4), scales=w_scales[:], in_=w_words[:].rearrange("p n c -> p (n c)")
+        )
+
+        squares = const.tile([P, D], F32)
+
+        def sum_squares(g, t):
+            nc.scalar.activation(
+                out=squares[:], in_=h[g][:, t, :], func=ACT.Square, accum_out=sum_sq[g][:, t : t + 1]
+            )
+
+        def clamp(g, t):
+            nc.scalar.activation(
+                out=excess[g][:, t : t + 1], in_=sum_sq[g][:, t : t + 1], func=ACT.Relu, bias=-EPS * EPS
+            )
+
+        def invert(g, t):
+            nc.scalar.activation(
+                out=inv_norm[g][:, t : t + 1],
+                in_=excess[g][:, t : t + 1],
+                func=ACT.Abs_reciprocal_sqrt,
+                scale=float(D),
+                bias=float(D) * EPS * EPS,
+            )
+
+        def scale_rows(g, t):
+            nc.scalar.activation(
+                out=h_unit[g][:, t, :], in_=h[g][:, t, :], func=ACT.Copy, scale=inv_norm[g][:, t : t + 1]
+            )
+
+        def normalise(g):
+            sum_sq[g] = stats.tile([P, TILES], F32, name="sum_sq")
+            excess[g] = stats.tile([P, TILES], F32, name="excess")
+            inv_norm[g] = stats.tile([P, TILES], F32, name="inv_norm")
+            h_unit[g] = scaled.tile([P, TILES, D], F32, name="h_unit")
+            for i in range(2 * TILES):
+                if i < TILES:
+                    sum_squares(g, i)
+                else:
+                    scale_rows(g, i - TILES)
+                if 1 <= i <= TILES:
+                    clamp(g, i - 1)
+                if 2 <= i <= TILES + 1:
+                    invert(g, i - 2)
+
+        def transpose(g):
+            h_turned[g] = []
+            for t in range(TILES):
+                bank = turned.tile([P, PACK, P], F32, tag="turned", name="h_turned")
+                for c in range(PACK):
+                    nc.tensor.transpose(bank[:, c, :], h_unit[g][:, t, c:D:PACK], ident_f32[:])
+                h_turned[g].append(bank)
+
+        def apply_gain(g):
+            hn_words[g] = packed.tile([P, TILES, P, PACK], BF16, name="hn_words", align_bytes=64)
+            for t in range(TILES):
+                nc.vector.tensor_tensor(
+                    out=hn_words[g][:, t, :, :],
+                    in0=h_turned[g][t][:].rearrange("p c r -> p r c"),
+                    in1=gain_by_k[:].unsqueeze(1).to_broadcast([P, P, PACK]),
+                    op=ALU.mult,
+                )
+
+        def quantise(g):
+            hn_codes[g] = packed.tile([P, TILES * P], U32, name="hn_codes", align_bytes=64)
+            hn_scales[g] = packed.tile([P, TILES * P], U8, name="hn_scales", align_bytes=64)
+            nc.vector.quantize_mx(
+                out=hn_codes[g][:].bitcast(FP8X4),
+                scales=hn_scales[g][:],
+                in_=hn_words[g][:].rearrange("p t r c -> p (t r c)"),
+            )
+
+        def multiply(g):
+            v_sums[g] = []
+            for t in range(TILES):
+                acc = products.tile([P, D], F32, tag="products", name="v_sums")
+                nc.tensor.matmul_mx(
+                    out=acc[:],
+                    lhsT=hn_codes[g][:, t * P : (t + 1) * P].bitcast(FP8X4),
+                    lhsT_scale=hn_scales[g][:, t * P : (t + 1) * P],
+                    rhs=w_codes[:].bitcast(FP8X4),
+                    rhs_scale=w_scales[:],
+                    start=True,
+                    stop=True,
+                )
+                v_sums[g].append(acc)
+
+        def add_bias_and_store(g):
+            v = results.tile([P, TILES, D], F32, name="v")
+            for t in range(TILES):
+                nc.vector.tensor_tensor(out=v[:, t, :], in0=v_sums[g][t][:], in1=bias_rows[:], op=ALU.add)
+                if (t + 1) % STORE_TILES == 0:
+                    part = slice(t + 1 - STORE_TILES, t + 1)
+                    nc.sync.dma_start(out=group_view(out, g)[:, part, :], in_=v[:, part, :])
+
+        def due(g):
+            return 0 <= g < GROUPS
+
+        for j in range(GROUPS + PRODUCT_LAG):
+            if due(j + LOADS_AHEAD):
+                load(j + LOADS_AHEAD)
+            if VECTOR_ADDS <= j < GROUPS:
+                add_inputs(j)
+            if due(j - PRODUCT_LAG):
+                quantise(j - PRODUCT_LAG)
+                multiply(j - PRODUCT_LAG)
+            if due(j - NORMALISE_LAG):
+                normalise(j - NORMALISE_LAG)
+                transpose(j - NORMALISE_LAG)
+            if due(j - GAIN_LAG):
+                apply_gain(j - GAIN_LAG)
+            if due(j - PRODUCT_LAG):
+                add_bias_and_store(j - PRODUCT_LAG)

@@ -13,6 +13,7 @@ ALU = mybir.AluOpType
 
 P = 128
 PACK = 4
+HALVES = 2
 D = P * PACK
 B = 8192
 EPS = 1e-12
@@ -53,11 +54,12 @@ def tile_recurrenttransformerblock_pa_t_kernel(tc, x, state, g1, wv, bv, out):
         x_rows, s_rows, h, sum_sq, excess, inv_norm, h_unit, h_turned = {}, {}, {}, {}, {}, {}, {}, {}
         hn_words, hn_codes, hn_scales, v_sums = {}, {}, {}, {}
 
-        def load(g):
-            x_rows[g] = inputs.tile([P, TILES, D], BF16, name="x_rows")
-            s_rows[g] = inputs.tile([P, TILES, D], BF16, name="s_rows")
-            nc.sync.dma_start(out=x_rows[g][:], in_=group_view(x, g))
-            nc.sync.dma_start(out=s_rows[g][:], in_=group_view(state, g))
+        def load(g, part=slice(0, TILES)):
+            if part.start == 0:
+                x_rows[g] = inputs.tile([P, TILES, D], BF16, name="x_rows")
+                s_rows[g] = inputs.tile([P, TILES, D], BF16, name="s_rows")
+            nc.sync.dma_start(out=x_rows[g][:, part, :], in_=group_view(x, g)[:, part, :])
+            nc.sync.dma_start(out=s_rows[g][:, part, :], in_=group_view(state, g)[:, part, :])
 
         def add_inputs(g):
             engine = nc.vector if g < VECTOR_ADDS else nc.gpsimd
@@ -68,45 +70,51 @@ def tile_recurrenttransformerblock_pa_t_kernel(tc, x, state, g1, wv, bv, out):
                     out=h[g][:, part, :], in0=x_rows[g][:, part, :], in1=s_rows[g][:, part, :], op=ALU.add
                 )
 
-        for g in range(LOADS_AHEAD):
+        w_rows = const.tile([P, PACK, D], BF16)
+        g_words = const.tile([P, PACK], BF16)
+        bias_rows = const.tile([P, D], BF16)
+        load(0, slice(0, ADD_TILES))
+        load(0, slice(ADD_TILES, TILES))
+        nc.sync.dma_start(out=w_rows[:], in_=wv.rearrange("(b p) k -> p b k", p=P))
+        nc.sync.dma_start(out=g_words[:], in_=g1.rearrange("(p c) -> p c", c=PACK))
+        for g in range(1, LOADS_AHEAD):
             load(g)
+        nc.sync.dma_start(out=bias_rows[:], in_=bv.partition_broadcast(P))
 
         ident_f32 = const.tile([P, P], F32)
         make_identity(nc, ident_f32[:])
-        ident_bf16 = const.tile([P, P], BF16)
-        make_identity(nc, ident_bf16[:])
 
         one = const.tile([P, 1], F32)
         nc.vector.memset(one[:], 1.0)
         warm = const.tile([P, 1], F32)
         nc.scalar.activation(out=warm[:], in_=one[:], func=ACT.Abs_reciprocal_sqrt)
 
-        g_words = const.tile([P, PACK], BF16)
-        nc.sync.dma_start(out=g_words[:], in_=g1.rearrange("(p c) -> p c", c=PACK))
-        w_rows = const.tile([P, PACK, D], BF16)
-        nc.sync.dma_start(out=w_rows[:], in_=wv.rearrange("(b p) k -> p b k", p=P))
-        bias_rows = const.tile([P, D], BF16)
-        nc.sync.dma_start(out=bias_rows[:], in_=bv.partition_broadcast(P))
-
-        for g in range(VECTOR_ADDS):
-            add_inputs(g)
-
-        gain_by_k = const.tile([P, PACK], F32)
-        nc.vector.tensor_copy(out=gain_by_k[:], in_=g_words[:])
+        add_inputs(0)
 
         w_words = const.tile([P, D, PACK], BF16, align_bytes=64)
-        for b in range(PACK):
-            w_turned = turned.tile([P, PACK, P], BF16, tag="turned")
-            for c in range(PACK):
-                nc.tensor.transpose(w_turned[:, c, :], w_rows[:, b, c:D:PACK], ident_bf16[:])
+        pairs_out = w_words[:].rearrange("p n c -> p (n c)").bitcast(F32)
+        for first in range(0, PACK, HALVES):
+            bank = turned.tile([P, HALVES, HALVES, P], F32, tag="turned", name="w_turned")
+            for i in range(HALVES):
+                pairs_in = w_rows[:, first + i, :].bitcast(F32)
+                for u in range(HALVES):
+                    nc.tensor.transpose(bank[:, i, u, :], pairs_in[:, u : D // 2 : HALVES], ident_f32[:])
+            span = slice(first * P * HALVES, (first + HALVES) * P * HALVES)
             nc.vector.tensor_copy(
-                out=w_words[:, b * P : (b + 1) * P, :], in_=w_turned[:].rearrange("p c n -> p n c")
+                out=pairs_out[:, span].rearrange("p (i r u) -> p i r u", i=HALVES, u=HALVES),
+                in_=bank[:].rearrange("p i u r -> p i r u"),
             )
         w_codes = const.tile([P, D], U32, align_bytes=64)
         w_scales = const.tile([P, D], U8, align_bytes=64)
         nc.vector.quantize_mx(
             out=w_codes[:].bitcast(FP8X4), scales=w_scales[:], in_=w_words[:].rearrange("p n c -> p (n c)")
         )
+
+        gain_by_k = const.tile([P, PACK], F32)
+        nc.vector.tensor_copy(out=gain_by_k[:], in_=g_words[:])
+
+        for g in range(1, VECTOR_ADDS):
+            add_inputs(g)
 
         squares = const.tile([P, D], F32)
 
@@ -195,6 +203,8 @@ def tile_recurrenttransformerblock_pa_t_kernel(tc, x, state, g1, wv, bv, out):
             v = results.tile([P, TILES, D], F32, name="v")
             for t in range(TILES):
                 nc.vector.tensor_tensor(out=v[:, t, :], in0=v_sums[g][t][:], in1=bias_rows[:], op=ALU.add)
+                if t == 0 and g == GROUPS - 2:
+                    quantise(GROUPS - 1)
                 if (t + 1) % STORE_TILES == 0:
                     part = slice(t + 1 - STORE_TILES, t + 1)
                     nc.sync.dma_start(out=group_view(out, g)[:, part, :], in_=v[:, part, :])
@@ -208,7 +218,8 @@ def tile_recurrenttransformerblock_pa_t_kernel(tc, x, state, g1, wv, bv, out):
             if VECTOR_ADDS <= j < GROUPS:
                 add_inputs(j)
             if due(j - PRODUCT_LAG):
-                quantise(j - PRODUCT_LAG)
+                if j - PRODUCT_LAG < GROUPS - 1:
+                    quantise(j - PRODUCT_LAG)
                 multiply(j - PRODUCT_LAG)
             if due(j - NORMALISE_LAG):
                 normalise(j - NORMALISE_LAG)

@@ -22,7 +22,7 @@ GROUP_ROWS = P * TILES
 GROUPS = B // GROUP_ROWS
 LOADS_AHEAD = 4
 ADD_TILES = 2
-VECTOR_ADDS = 3
+VECTOR_ADDS = 2
 STORE_TILES = 2
 
 NORMALISE_LAG = 1
@@ -45,6 +45,7 @@ def tile_recurrenttransformerblock_pa_t_kernel(tc, x, state, g1, wv, bv, out):
         sums = ctx.enter_context(tc.tile_pool(name="sums", bufs=3))
         stats = ctx.enter_context(tc.tile_pool(name="stats", bufs=3))
         results = ctx.enter_context(tc.tile_pool(name="results", bufs=3))
+        unused = ctx.enter_context(tc.tile_pool(name="unused", bufs=3))
         scaled = ctx.enter_context(tc.tile_pool(name="scaled", bufs=2))
         packed = ctx.enter_context(tc.tile_pool(name="packed", bufs=2))
         turned = ctx.enter_context(tc.psum_pool(name="turned", bufs=TILES))
@@ -116,9 +117,8 @@ def tile_recurrenttransformerblock_pa_t_kernel(tc, x, state, g1, wv, bv, out):
         for g in range(1, VECTOR_ADDS):
             add_inputs(g)
 
-        squares = const.tile([P, D], F32)
-
         def sum_squares(g, t):
+            squares = unused.tile([P, D], F32, name="squares")
             nc.scalar.activation(
                 out=squares[:], in_=h[g][:, t, :], func=ACT.Square, accum_out=sum_sq[g][:, t : t + 1]
             )

@@ -24,6 +24,8 @@ LOADS_AHEAD = 4
 ADD_TILES = 2
 VECTOR_ADDS = 2
 STORE_TILES = 2
+RELAYED_GROUP = GROUPS - 3
+RELAYED_TILES = 2
 
 NORMALISE_LAG = 1
 GAIN_LAG = 2
@@ -46,6 +48,7 @@ def tile_recurrenttransformerblock_pa_t_kernel(tc, x, state, g1, wv, bv, out):
         stats = ctx.enter_context(tc.tile_pool(name="stats", bufs=3))
         results = ctx.enter_context(tc.tile_pool(name="results", bufs=3))
         unused = ctx.enter_context(tc.tile_pool(name="unused", bufs=3))
+        copies = ctx.enter_context(tc.tile_pool(name="copies", bufs=RELAYED_TILES))
         scaled = ctx.enter_context(tc.tile_pool(name="scaled", bufs=2))
         packed = ctx.enter_context(tc.tile_pool(name="packed", bufs=2))
         turned = ctx.enter_context(tc.psum_pool(name="turned", bufs=TILES))
@@ -63,10 +66,14 @@ def tile_recurrenttransformerblock_pa_t_kernel(tc, x, state, g1, wv, bv, out):
             nc.sync.dma_start(out=s_rows[g][:, part, :], in_=group_view(state, g)[:, part, :])
 
         def add_inputs(g):
-            engine = nc.vector if g < VECTOR_ADDS else nc.gpsimd
             h[g] = sums.tile([P, TILES, D], F32, name="h")
-            for t in range(0, TILES, ADD_TILES):
-                part = slice(t, t + ADD_TILES)
+            if g == VECTOR_ADDS:
+                shares = [(nc.vector, 0, 1), (nc.gpsimd, 1, TILES)]
+            else:
+                engine = nc.vector if g < VECTOR_ADDS else nc.gpsimd
+                shares = [(engine, t, t + ADD_TILES) for t in range(0, TILES, ADD_TILES)]
+            for engine, first, end in shares:
+                part = slice(first, end)
                 engine.tensor_tensor(
                     out=h[g][:, part, :], in0=x_rows[g][:, part, :], in1=s_rows[g][:, part, :], op=ALU.add
                 )
@@ -76,7 +83,11 @@ def tile_recurrenttransformerblock_pa_t_kernel(tc, x, state, g1, wv, bv, out):
         bias_rows = const.tile([P, D], BF16)
         load(0, slice(0, ADD_TILES))
         load(0, slice(ADD_TILES, TILES))
-        nc.sync.dma_start(out=w_rows[:], in_=wv.rearrange("(b p) k -> p b k", p=P))
+        for first in range(0, PACK, HALVES):
+            nc.sync.dma_start(
+                out=w_rows[:, first : first + HALVES, :],
+                in_=wv[first * P : (first + HALVES) * P, :].rearrange("(b p) k -> p b k", p=P),
+            )
         nc.sync.dma_start(out=g_words[:], in_=g1.rearrange("(p c) -> p c", c=PACK))
         for g in range(1, LOADS_AHEAD):
             load(g)
@@ -201,8 +212,14 @@ def tile_recurrenttransformerblock_pa_t_kernel(tc, x, state, g1, wv, bv, out):
 
         def add_bias_and_store(g):
             v = results.tile([P, TILES, D], F32, name="v")
+            own = TILES - RELAYED_TILES if g == RELAYED_GROUP else TILES
+            for t in range(own, TILES):
+                copy = copies.tile([P, D], F32, name="copy")
+                nc.scalar.copy(out=copy[:], in_=v_sums[g][t][:])
+                nc.gpsimd.tensor_tensor(out=v[:, t, :], in0=copy[:], in1=bias_rows[:], op=ALU.add)
             for t in range(TILES):
-                nc.vector.tensor_tensor(out=v[:, t, :], in0=v_sums[g][t][:], in1=bias_rows[:], op=ALU.add)
+                if t < own:
+                    nc.vector.tensor_tensor(out=v[:, t, :], in0=v_sums[g][t][:], in1=bias_rows[:], op=ALU.add)
                 if t == 0 and g == GROUPS - 2:
                     quantise(GROUPS - 1)
                 if (t + 1) % STORE_TILES == 0:

@@ -44,7 +44,7 @@ def tile_recurrenttransformerblock_pa_t_kernel(tc, x, state, g1, wv, bv, out):
     with ExitStack() as ctx:
         const = ctx.enter_context(tc.tile_pool(name="const", bufs=1))
         inputs = ctx.enter_context(tc.tile_pool(name="inputs", bufs=LOADS_AHEAD + 1))
-        sums = ctx.enter_context(tc.tile_pool(name="sums", bufs=3))
+        sums = ctx.enter_context(tc.tile_pool(name="sums", bufs=2))
         stats = ctx.enter_context(tc.tile_pool(name="stats", bufs=3))
         results = ctx.enter_context(tc.tile_pool(name="results", bufs=3))
         unused = ctx.enter_context(tc.tile_pool(name="unused", bufs=3))
@@ -67,11 +67,12 @@ def tile_recurrenttransformerblock_pa_t_kernel(tc, x, state, g1, wv, bv, out):
 
         def add_inputs(g):
             h[g] = sums.tile([P, TILES, D], F32, name="h")
-            if g == VECTOR_ADDS:
+            if g < VECTOR_ADDS:
+                shares = [(nc.vector, t, t + ADD_TILES) for t in range(0, TILES, ADD_TILES)]
+            elif g == VECTOR_ADDS:
                 shares = [(nc.vector, 0, 1), (nc.gpsimd, 1, TILES)]
             else:
-                engine = nc.vector if g < VECTOR_ADDS else nc.gpsimd
-                shares = [(engine, t, t + ADD_TILES) for t in range(0, TILES, ADD_TILES)]
+                shares = [(nc.gpsimd, 0, TILES)]
             for engine, first, end in shares:
                 part = slice(first, end)
                 engine.tensor_tensor(

@@ -25,7 +25,7 @@ ADD_TILES = 2
 VECTOR_ADDS = 2
 STORE_TILES = 2
 RELAYED_GROUP = GROUPS - 3
-RELAYED_TILES = 2
+RELAYED_TILES = 1
 
 NORMALISE_LAG = 1
 GAIN_LAG = 2
@@ -89,7 +89,7 @@ def tile_recurrenttransformerblock_pa_t_kernel(tc, x, state, g1, wv, bv, out):
                 out=w_rows[:, first : first + HALVES, :],
                 in_=wv[first * P : (first + HALVES) * P, :].rearrange("(b p) k -> p b k", p=P),
             )
-        nc.sync.dma_start(out=g_words[:], in_=g1.rearrange("(p c) -> p c", c=PACK))
+        nc.scalar.dma_start(out=g_words[:], in_=g1.rearrange("(p c) -> p c", c=PACK))
         for g in range(1, LOADS_AHEAD):
             load(g)
         nc.sync.dma_start(out=bias_rows[:], in_=bv.partition_broadcast(P))

from contextlib import ExitStack

import concourse.mybir as mybir
from concourse.masks import make_identity

F32 = mybir.dt.float32
BF16 = mybir.dt.bfloat16
U32 = mybir.dt.uint32
U8 = mybir.dt.uint8
FP8X4 = mybir.dt.float8_e4m3fn_x4
ACT = mybir.ActivationFunctionType
ALU = mybir.AluOpType

P = 128
PACK = 4
HALVES = 2
D = P * PACK
B = 8192
EPS = 1e-12
TILES = 4
GROUP_ROWS = P * TILES
GROUPS = B // GROUP_ROWS
LOADS_AHEAD = 4
ADD_TILES = 2
VECTOR_ADDS = 2
STORE_TILES = 2
RELAYED_GROUP = GROUPS - 3
RELAYED_TILES = 1

NORMALISE_LAG = 1
GAIN_LAG = 2
PRODUCT_LAG = 3

FLOPS = 2 * B * D * D


def tile_recurrenttransformerblock_pa_t_kernel(tc, x, state, g1, wv, bv, out):
    nc = tc.nc

    def group_view(dram, g):
        rows = dram[g * GROUP_ROWS : (g + 1) * GROUP_ROWS, :]
        return rows.rearrange("(p t) k -> p t k", t=TILES)

    with ExitStack() as ctx:
        const = ctx.enter_context(tc.tile_pool(name="const", bufs=1))
        inputs = ctx.enter_context(tc.tile_pool(name="inputs", bufs=LOADS_AHEAD + 1))
        sums = ctx.enter_context(tc.tile_pool(name="sums", bufs=2))
        stats = ctx.enter_context(tc.tile_pool(name="stats", bufs=3))
        results = ctx.enter_context(tc.tile_pool(name="results", bufs=3))
        unused = ctx.enter_context(tc.tile_pool(name="unused", bufs=3))
        copies = ctx.enter_context(tc.tile_pool(name="copies", bufs=RELAYED_TILES))
        scaled = ctx.enter_context(tc.tile_pool(name="scaled", bufs=2))
        packed = ctx.enter_context(tc.tile_pool(name="packed", bufs=2))
        turned = ctx.enter_context(tc.psum_pool(name="turned", bufs=TILES))
        products = ctx.enter_context(tc.psum_pool(name="products", bufs=TILES))
        ctx.enter_context(tc.manual_schedule())

        x_rows, s_rows, h, sum_sq, excess, inv_norm, h_unit, h_turned = {}, {}, {}, {}, {}, {}, {}, {}
        hn_words, hn_codes, hn_scales, v_sums = {}, {}, {}, {}

        def load(g, part=slice(0, TILES)):
            if part.start == 0:
                x_rows[g] = inputs.tile([P, TILES, D], BF16, name="x_rows")
                s_rows[g] = inputs.tile([P, TILES, D], BF16, name="s_rows")
            nc.sync.dma_start(out=x_rows[g][:, part, :], in_=group_view(x, g)[:, part, :])
            nc.sync.dma_start(out=s_rows[g][:, part, :], in_=group_view(state, g)[:, part, :])

        def add_inputs(g):
            h[g] = sums.tile([P, TILES, D], F32, name="h")
            if g < VECTOR_ADDS:
                shares = [(nc.vector, t, t + ADD_TILES) for t in range(0, TILES, ADD_TILES)]
            elif g == VECTOR_ADDS:
                shares = [(nc.vector, 0, 1), (nc.gpsimd, 1, TILES)]
            else:
                shares = [(nc.gpsimd, 0, TILES)]
            for engine, first, end in shares:
                part = slice(first, end)
                engine.tensor_tensor(
                    out=h[g][:, part, :], in0=x_rows[g][:, part, :], in1=s_rows[g][:, part, :], op=ALU.add
                )

        w_rows = const.tile([P, PACK, D], BF16)
        g_words = const.tile([P, PACK], BF16)
        bias_rows = const.tile([P, D], BF16)
        load(0, slice(0, ADD_TILES))
        load(0, slice(ADD_TILES, TILES))
        for first in range(0, PACK, HALVES):
            nc.sync.dma_start(
                out=w_rows[:, first : first + HALVES, :],
                in_=wv[first * P : (first + HALVES) * P, :].rearrange("(b p) k -> p b k", p=P),
            )
        nc.scalar.dma_start(out=g_words[:], in_=g1.rearrange("(p c) -> p c", c=PACK))
        for g in range(1, LOADS_AHEAD):
            load(g)
        nc.sync.dma_start(out=bias_rows[:], in_=bv.partition_broadcast(P))

        ident_f32 = const.tile([P, P], F32)
        make_identity(nc, ident_f32[:])

        one = const.tile([P, 1], F32)
        nc.vector.memset(one[:], 1.0)
        warm = const.tile([P, 1], F32)
        nc.scalar.activation(out=warm[:], in_=one[:], func=ACT.Abs_reciprocal_sqrt)

        add_inputs(0)

        w_words = const.tile([P, D, PACK], BF16, align_bytes=64)
        pairs_out = w_words[:].rearrange("p n c -> p (n c)").bitcast(F32)
        for first in range(0, PACK, HALVES):
            bank = turned.tile([P, HALVES, HALVES, P], F32, tag="turned", name="w_turned")
            for i in range(HALVES):
                pairs_in = w_rows[:, first + i, :].bitcast(F32)
                for u in range(HALVES):
                    nc.tensor.transpose(bank[:, i, u, :], pairs_in[:, u : D // 2 : HALVES], ident_f32[:])
            span = slice(first * P * HALVES, (first + HALVES) * P * HALVES)
            nc.vector.tensor_copy(
                out=pairs_out[:, span].rearrange("p (i r u) -> p i r u", i=HALVES, u=HALVES),
                in_=bank[:].rearrange("p i u r -> p i r u"),
            )
        w_codes = const.tile([P, D], U32, align_bytes=64)
        w_scales = const.tile([P, D], U8, align_bytes=64)
        nc.vector.quantize_mx(
            out=w_codes[:].bitcast(FP8X4), scales=w_scales[:], in_=w_words[:].rearrange("p n c -> p (n c)")
        )

        gain_by_k = const.tile([P, PACK], F32)
        nc.vector.tensor_copy(out=gain_by_k[:], in_=g_words[:])

        for g in range(1, VECTOR_ADDS):
            add_inputs(g)

        def sum_squares(g, t):
            squares = unused.tile([P, D], F32, name="squares")
            nc.scalar.activation(
                out=squares[:], in_=h[g][:, t, :], func=ACT.Square, accum_out=sum_sq[g][:, t : t + 1]
            )

        def clamp(g, t):
            nc.scalar.activation(
                out=excess[g][:, t : t + 1], in_=sum_sq[g][:, t : t + 1], func=ACT.Relu, bias=-EPS * EPS
            )

        def invert(g, t):
            nc.scalar.activation(
                out=inv_norm[g][:, t : t + 1],
                in_=excess[g][:, t : t + 1],
                func=ACT.Abs_reciprocal_sqrt,
                scale=float(D),
                bias=float(D) * EPS * EPS,
            )

        def scale_rows(g, t):
            nc.scalar.activation(
                out=h_unit[g][:, t, :], in_=h[g][:, t, :], func=ACT.Copy, scale=inv_norm[g][:, t : t + 1]
            )

        def normalise(g):
            sum_sq[g] = stats.tile([P, TILES], F32, name="sum_sq")
            excess[g] = stats.tile([P, TILES], F32, name="excess")
            inv_norm[g] = stats.tile([P, TILES], F32, name="inv_norm")
            h_unit[g] = scaled.tile([P, TILES, D], F32, name="h_unit")
            for i in range(2 * TILES):
                if i < TILES:
                    sum_squares(g, i)
                else:
                    scale_rows(g, i - TILES)
                if 1 <= i <= TILES:
                    clamp(g, i - 1)
                if 2 <= i <= TILES + 1:
                    invert(g, i - 2)

        def transpose(g):
            h_turned[g] = []
            for t in range(TILES):
                bank = turned.tile([P, PACK, P], F32, tag="turned", name="h_turned")
                for c in range(PACK):
                    nc.tensor.transpose(bank[:, c, :], h_unit[g][:, t, c:D:PACK], ident_f32[:])
                h_turned[g].append(bank)

        def apply_gain(g):
            hn_words[g] = packed.tile([P, TILES, P, PACK], BF16, name="hn_words", align_bytes=64)
            for t in range(TILES):
                nc.vector.tensor_tensor(
                    out=hn_words[g][:, t, :, :],
                    in0=h_turned[g][t][:].rearrange("p c r -> p r c"),
                    in1=gain_by_k[:].unsqueeze(1).to_broadcast([P, P, PACK]),
                    op=ALU.mult,
                )

        def quantise(g):
            hn_codes[g] = packed.tile([P, TILES * P], U32, name="hn_codes", align_bytes=64)
            hn_scales[g] = packed.tile([P, TILES * P], U8, name="hn_scales", align_bytes=64)
            nc.vector.quantize_mx(
                out=hn_codes[g][:].bitcast(FP8X4),
                scales=hn_scales[g][:],
                in_=hn_words[g][:].rearrange("p t r c -> p (t r c)"),
            )

        def multiply(g):
            v_sums[g] = []
            for t in range(TILES):
                acc = products.tile([P, D], F32, tag="products", name="v_sums")
                nc.tensor.matmul_mx(
                    out=acc[:],
                    lhsT=hn_codes[g][:, t * P : (t + 1) * P].bitcast(FP8X4),
                    lhsT_scale=hn_scales[g][:, t * P : (t + 1) * P],
                    rhs=w_codes[:].bitcast(FP8X4),
                    rhs_scale=w_scales[:],
                    start=True,
                    stop=True,
                )
                v_sums[g].append(acc)

        def add_bias_and_store(g):
            v = results.tile([P, TILES, D], F32, name="v")
            own = TILES - RELAYED_TILES if g == RELAYED_GROUP else TILES
            for t in range(own, TILES):
                copy = copies.tile([P, D], F32, name="copy")
                nc.scalar.copy(out=copy[:], in_=v_sums[g][t][:])
                nc.gpsimd.tensor_tensor(out=v[:, t, :], in0=copy[:], in1=bias_rows[:], op=ALU.add)
            for t in range(TILES):
                if t < own:
                    nc.vector.tensor_tensor(out=v[:, t, :], in0=v_sums[g][t][:], in1=bias_rows[:], op=ALU.add)
                if t == 0 and g == GROUPS - 2:
                    quantise(GROUPS - 1)
                if (t + 1) % STORE_TILES == 0:
                    part = slice(t + 1 - STORE_TILES, t + 1)
                    nc.sync.dma_start(out=group_view(out, g)[:, part, :], in_=v[:, part, :])

        def due(g):
            return 0 <= g < GROUPS

        for j in range(GROUPS + PRODUCT_LAG):
            if due(j + LOADS_AHEAD):
                load(j + LOADS_AHEAD)
            if VECTOR_ADDS <= j < GROUPS:
                add_inputs(j)
            if due(j - PRODUCT_LAG):
                if j - PRODUCT_LAG < GROUPS - 1:
                    quantise(j - PRODUCT_LAG)
                multiply(j - PRODUCT_LAG)
            if due(j - NORMALISE_LAG):
                normalise(j - NORMALISE_LAG)
                transpose(j - NORMALISE_LAG)
            if due(j - GAIN_LAG):
                apply_gain(j - GAIN_LAG)
            if due(j - PRODUCT_LAG):
                add_bias_and_store(j - PRODUCT_LAG)
